import numpy as np
import ml_dtypes


def mxq(x, axis, fmt="e4m3"):
    dtype, down = {"e4m3": (ml_dtypes.float8_e4m3fn, 7), "e5m2": (ml_dtypes.float8_e5m2, 14)}[fmt]
    v = np.moveaxis(np.asarray(x, np.float32).astype(ml_dtypes.bfloat16).astype(np.float64), axis, -1)
    blocks = v.reshape(v.shape[:-1] + (-1, 32))
    amax = np.abs(blocks).max(-1, keepdims=True)
    byte = np.maximum(np.where(amax > 0, np.frexp(amax)[1] - 1 + 127, 0) - down, 1)
    scale = np.exp2(byte - 127.0)
    codes = (blocks / scale).astype(np.float32).astype(dtype).astype(np.float64)
    return np.moveaxis((codes * scale).reshape(v.shape), -1, axis)


WIDE = False


def mx_kscale(k):
    if not WIDE:
        return np.ones(k)
    levels = np.array([10, -10, 5, -5, 0])
    a = np.random.permutation(np.resize(levels, k // 512 * 4)).reshape(k // 512, 4)
    idx = np.arange(k)
    return np.exp2(a[idx // 512, idx % 128 // 32])


BF16 = ml_dtypes.bfloat16


def bf(x):
    return np.asarray(x, np.float32).astype(BF16)


def f64(x):
    return np.asarray(x).astype(np.float64)


B, DIN, DOUT = 16384, 512, 128

MIN_NORM = 1e-15
PROJ_EPS = 1e-3
W_MUL = 0.1
B_MUL = 0.1
C = 1.0


def artanh(x):
    x = np.clip(x, -1.0 + 1e-5, 1.0 - 1e-5)
    return 0.5 * (np.log1p(x) - np.log1p(-x))


def mobius_matvec(w, x, c):
    sqrt_c = c ** 0.5
    x_norm = np.maximum(np.linalg.norm(x, axis=-1, keepdims=True), MIN_NORM)
    mx = mxq(x, 1, "e4m3") @ mxq(w, 1, "e4m3").T
    mx_norm = np.maximum(np.linalg.norm(mx, axis=-1, keepdims=True), MIN_NORM)
    res = np.tanh(mx_norm / x_norm * artanh(sqrt_c * x_norm)) * mx / (mx_norm * sqrt_c)
    zero_row = np.all(mx == 0, axis=-1, keepdims=True)
    return np.where(zero_row, 0.0, res)


def expmap0(u, c):
    sqrt_c = c ** 0.5
    u_norm = np.maximum(np.linalg.norm(u, axis=-1, keepdims=True), MIN_NORM)
    return np.tanh(sqrt_c * u_norm) * u / (sqrt_c * u_norm)


def mobius_add(x, y, c):
    x2 = np.sum(x * x, axis=-1, keepdims=True)
    y2 = np.sum(y * y, axis=-1, keepdims=True)
    xy = np.sum(x * y, axis=-1, keepdims=True)
    num = (1 + 2 * c * xy + c * y2) * x + (1 - c * x2) * y
    denom = 1 + 2 * c * xy + c * c * x2 * y2
    return num / np.maximum(denom, MIN_NORM)


def project(x, c):
    sqrt_c = c ** 0.5
    norm = np.maximum(np.linalg.norm(x, axis=-1, keepdims=True), MIN_NORM)
    maxnorm = (1.0 - PROJ_EPS) / sqrt_c
    return np.where(norm > maxnorm, x / norm * maxnorm, x)


def setup_inputs():
    s = mx_kscale(DIN)
    g = np.exp2(np.ceil(np.log2(np.sqrt(np.mean(s * s)))))
    return {"x": bf(np.random.standard_normal((B, DIN)) * 0.7 / np.sqrt(DIN) * s / g),
            "weight": bf(np.random.standard_normal((DOUT, DIN)) * 10.0 / np.sqrt(DOUT) * g / s),
            "bias": bf(np.random.standard_normal(DOUT) * 3.0 / np.sqrt(DOUT))}


def reference(x, weight, bias):
    c = C
    w_lr = f64(weight) * W_MUL
    mv = mobius_matvec(w_lr, f64(x), c)
    b = expmap0(f64(bias) * B_MUL, c)
    out = project(mobius_add(mv, b[None, :], 1.0), c)
    return np.where(out >= 0, out, 0.2 * out)

@@ -1,0 +1,440 @@
+from contextlib import ExitStack
+
+import concourse.mybir as mybir
+from concourse.masks import make_identity
+
+FLOPS = 2 * 16384 * 512 * 128
+
+F32 = mybir.dt.float32
+BF16 = mybir.dt.bfloat16
+U32 = mybir.dt.uint32
+U8 = mybir.dt.uint8
+FP8X4 = mybir.dt.float8_e4m3fn_x4
+ALU = mybir.AluOpType
+ACT = mybir.ActivationFunctionType
+
+P = 128
+K = 512
+DOUT = 128
+NT = 128
+CH = 4
+NCH = NT // CH
+GROUPS = (32, 32, 32, 16, 8, 8)
+LOOKAHEAD = 4
+
+
+def tile_hypequalizedlinear_t_kernel(tc, x, weight, bias, out):
+    nc = tc.nc
+    xv = x.rearrange("(p t) k -> p t k", t=NT)
+    ov = out.rearrange("(p t) o -> p t o", t=NT)
+    with ExitStack() as ctx:
+        const = ctx.enter_context(tc.tile_pool(name="const", bufs=1))
+        xpool = ctx.enter_context(tc.tile_pool(name="xpool", bufs=6))
+        gpool = ctx.enter_context(tc.tile_pool(name="gpool", bufs=3))
+        bpool = ctx.enter_context(tc.tile_pool(name="bpool", bufs=3))
+        ypool = ctx.enter_context(tc.tile_pool(name="ypool", bufs=4))
+        ps_xt = ctx.enter_context(tc.psum_pool(name="ps_xt", bufs=2))
+        ps_ms = ctx.enter_context(tc.psum_pool(name="ps_ms", bufs=2))
+        ps_mv = ctx.enter_context(tc.psum_pool(name="ps_mv", bufs=2))
+        ps_m2 = ctx.enter_context(tc.psum_pool(name="ps_m2", bufs=2))
+
+        ctx.enter_context(tc.manual_schedule())
+        v = nc.vector
+        sc = nc.scalar
+
+        def col(name):
+            return const.tile([P, 1], F32, name=name)
+
+        def wide(name, n=1):
+            if n == 1:
+                return const.tile([P, NT], F32, name=name)
+            return const.tile([P, n, NT], F32, name=name)
+
+        ident = const.tile([P, P], F32, name="ident")
+        half = col("half")
+        w_raw = const.tile([P, K], BF16, name="w_raw")
+        bias_bc = const.tile([P, DOUT], BF16, name="bias_bc")
+        junk_c = const.tile([P, K], BF16, name="junk_c")
+        junk_d = const.tile([P, DOUT], F32, name="junk_d")
+        junk_e = const.tile([P, DOUT], F32, name="junk_e")
+        w_grouped = const.tile([P, K], BF16, name="w_grouped", align_bytes=64)
+        w_codes = const.tile([P, DOUT], U32, name="w_codes", align_bytes=64)
+        w_scales = const.tile([P, DOUT], U8, name="w_scales", align_bytes=64)
+        u_f = const.tile([P, DOUT], F32, name="u_f")
+        b_pos = const.tile([P, DOUT], F32, name="b_pos")
+        b_neg = const.tile([P, DOUT], F32, name="b_neg")
+        un2 = col("un2")
+        un2c = col("un2c")
+        un = col("un")
+        th = col("th")
+        run = col("run")
+        kk = col("kk")
+        y2 = col("y2")
+        ym1 = col("ym1")
+        codes = const.tile([P, NT * P], U32, name="codes", align_bytes=64)
+        scales = const.tile([P, NT * P], U8, name="scales", align_bytes=64)
+        s2 = wide("s2", 2)
+        pb = wide("pb")
+        al = wide("al")
+        nbe = wide("nbe")
+        c_s2c = wide("c_s2c", 2)
+        c_nrm = wide("c_nrm", 2)
+        c_rnrm = wide("c_rnrm", 2)
+        c_nv = wide("c_nv")
+        c_dn = wide("c_dn")
+        c_rdn = wide("c_rdn")
+        c_base = wide("c_base")
+        c_r = wide("c_r")
+        c_e = wide("c_e")
+        c_e1 = wide("c_e1")
+        c_re = wide("c_re")
+        c_t = wide("c_t")
+        c_s = wide("c_s")
+        c_x2 = wide("c_x2")
+        c_xy = wide("c_xy")
+        c_c1 = wide("c_c1")
+        c_den = wide("c_den")
+        c_denc = wide("c_denc")
+        c_rden = wide("c_rden")
+        c_num = wide("c_num")
+        c_nn2 = wide("c_nn2")
+        c_nn2c = wide("c_nn2c")
+        c_nn = wide("c_nn")
+        c_rnn = wide("c_rnn")
+        c_f = wide("c_f")
+        c_rf = wide("c_rf")
+        c_as = wide("c_as")
+
+        xs_of = {}
+        xt_of = {}
+        g_of = {}
+        ms_of = {}
+        mv_of = {}
+        m2_of = {}
+        t1_of = {}
+        y_of = {}
+
+        def ts(o, i, s1, s2_, o0, o1=None):
+            if o1 is None:
+                return lambda: v.tensor_scalar(out=o, in0=i, scalar1=s1, scalar2=None, op0=o0)
+            return lambda: v.tensor_scalar(out=o, in0=i, scalar1=s1, scalar2=s2_, op0=o0, op1=o1)
+
+        def tt(o, i0, i1, op):
+            return lambda: v.tensor_tensor(out=o, in0=i0, in1=i1, op=op)
+
+        def stt(o, i0, s, i1, o0, o1, acc=None):
+            return lambda: v.scalar_tensor_tensor(out=o, in0=i0, scalar=s, in1=i1, op0=o0, op1=o1, accum_out=acc)
+
+        def rcp(o, i):
+            return lambda: v.reciprocal(out=o, in_=i)
+
+        def act(o, i, func, acc=None):
+            return lambda: sc.activation(out=o, in_=i, func=func, accum_out=acc)
+
+        def scaled(o, i, s):
+            return lambda: sc.activation(out=o, in_=i, func=ACT.Copy, scale=s)
+
+        def power(o, i0, i1):
+            return lambda: nc.gpsimd.tensor_tensor(out=o, in0=i0, in1=i1, op=ALU.pow)
+
+        def weave(bulk, extra, skip):
+            i = 0
+            for n, f in enumerate(bulk):
+                f()
+                if n >= skip and i < len(extra):
+                    extra[i]()
+                    i += 1
+            for f in extra[i:]:
+                f()
+
+        def mx(dst, t):
+            nc.tensor.matmul_mx(
+                out=dst,
+                lhsT=codes[:, t * P : (t + 1) * P].bitcast(FP8X4),
+                lhsT_scale=scales[:, t * P : (t + 1) * P],
+                rhs=w_codes[:].bitcast(FP8X4),
+                rhs_scale=w_scales[:],
+                start=True,
+                stop=True,
+            )
+
+        def load(blk, parts):
+            xs = xpool.tile([P, 2 * CH * K], BF16, name="xs")
+            xs_of[blk] = xs
+            n = 2 * CH // parts
+            for i in range(parts):
+                nc.sync.dma_start(
+                    out=xs[:, i * n * K : (i + 1) * n * K].rearrange("p (t k) -> p t k", k=K),
+                    in_=xv[:, blk * 2 * CH + i * n : blk * 2 * CH + (i + 1) * n, :],
+                )
+
+        def transposes(c):
+            xw = xs_of[c // 2][:].bitcast(F32)
+            banks = []
+            for h in range(2):
+                xt = ps_xt.tile([P, 512], F32, name="xt")
+                banks.append(xt)
+                for q in range(4):
+                    loc = (c % 2) * CH + 2 * h + q // 2
+                    w0 = loc * (K // 2) + (q % 2) * P
+                    nc.tensor.transpose(xt[:, q * P : (q + 1) * P], xw[:, w0 : w0 + P], ident[:])
+            xt_of[c] = banks
+
+        def copies(c, on_scalar):
+            g = gpool.tile([P, CH * K], BF16, name="g", align_bytes=64)
+            g_of[c] = g
+            gw = g[:].bitcast(F32)
+            for h in range(2):
+                dst = gw[:, h * 512 : (h + 1) * 512].rearrange("p (t r u) -> p t r u", t=2, u=2)
+                src = xt_of[c][h][:].rearrange("p (t u r) -> p t r u", t=2, u=2)
+                if h >= 2 - on_scalar:
+                    sc.copy(out=dst, in_=src)
+                else:
+                    v.tensor_copy(out=dst, in_=src)
+
+        def x_squares(c):
+            xs = xs_of[c // 2]
+            calls = []
+            for j in range(CH):
+                loc = (c % 2) * CH + j
+                t = c * CH + j
+                calls.append(act(junk_c[:], xs[:, loc * K : (loc + 1) * K], ACT.Square, s2[:, 0, t : t + 1]))
+            return calls
+
+        def quantise(c):
+            t0 = c * CH
+            v.quantize_mx(
+                out=codes[:, t0 * P : (t0 + CH) * P].bitcast(FP8X4),
+                scales=scales[:, t0 * P : (t0 + CH) * P],
+                in_=g_of[c][:],
+            )
+
+        def products(c, pool, name, keep):
+            bank = pool.tile([P, 512], F32, name=name)
+            keep[c] = bank
+            for j in range(CH):
+                mx(bank[:, j * P : (j + 1) * P], c * CH + j)
+
+        def m_squares(c):
+            return [
+                act(junk_d[:], ms_of[c][:, j * P : (j + 1) * P], ACT.Square, s2[:, 1, c * CH + j : c * CH + j + 1])
+                for j in range(CH)
+            ]
+
+        def m_dot_b(c):
+            return [
+                stt(
+                    junk_e[:],
+                    mv_of[c][:, j * P : (j + 1) * P],
+                    1.0,
+                    b_pos[:],
+                    ALU.mult,
+                    ALU.mult,
+                    pb[:, c * CH + j : c * CH + j + 1],
+                )
+                for j in range(CH)
+            ]
+
+        def store(c):
+            return lambda: nc.sync.dma_start(
+                out=ov[:, (c - 1) * CH : (c + 1) * CH, :],
+                in_=y_of[c // 2][:].rearrange("p (t o) -> p t o", o=DOUT),
+            )
+
+        def finish_scalar(c):
+            t1 = bpool.tile([P, CH * DOUT], F32, name="bb")
+            t1_of[c] = t1
+            return [
+                scaled(t1[:, j * P : (j + 1) * P], m2_of[c][:, j * P : (j + 1) * P], al[:, c * CH + j : c * CH + j + 1])
+                for j in range(CH)
+            ]
+
+        def finish_vector(c, with_scalar):
+            if c % 2 == 0:
+                y_of[c // 2] = ypool.tile([P, 2 * CH * DOUT], F32, name="y")
+            y = y_of[c // 2]
+            off = (c % 2) * CH * DOUT
+            calls = []
+            if with_scalar:
+                t1 = t1_of[c]
+                for j in range(CH):
+                    t = c * CH + j
+                    calls.append(
+                        stt(
+                            y[:, off + j * P : off + (j + 1) * P],
+                            b_neg[:],
+                            nbe[:, t : t + 1],
+                            t1[:, j * P : (j + 1) * P],
+                            ALU.mult,
+                            ALU.add,
+                        )
+                    )
+            else:
+                bb = bpool.tile([P, CH * DOUT], F32, name="bb")
+                for j in range(CH):
+                    t = c * CH + j
+                    calls.append(ts(bb[:, j * P : (j + 1) * P], b_neg[:], nbe[:, t : t + 1], None, ALU.mult))
+                for j in range(CH):
+                    t = c * CH + j
+                    calls.append(
+                        stt(
+                            y[:, off + j * P : off + (j + 1) * P],
+                            m2_of[c][:, j * P : (j + 1) * P],
+                            al[:, t : t + 1],
+                            bb[:, j * P : (j + 1) * P],
+                            ALU.mult,
+                            ALU.add,
+                        )
+                    )
+            ysl = y[:, off : off + CH * DOUT]
+            calls.append(stt(ysl, ysl, 0.2, ysl, ALU.mult, ALU.max))
+            if c % 2 == 1:
+                calls.append(store(c))
+            return calls
+
+        def chain(a, b):
+            sl = slice(a, b)
+            xn = c_nrm[:, 0, sl]
+            mn = c_nrm[:, 1, sl]
+            rxn = c_rnrm[:, 0, sl]
+            rmn = c_rnrm[:, 1, sl]
+            seg0 = [ts(c_s2c[:, :, sl], s2[:, :, sl], 1e-30, None, ALU.max)]
+            root1 = [act(c_nrm[:, :, sl], c_s2c[:, :, sl], ACT.Sqrt)]
+            seg1 = [
+                rcp(c_rnrm[:, :, sl], c_nrm[:, :, sl]),
+                ts(c_nv[:, sl], xn, 1.0 - 1e-5, -1.0, ALU.min, ALU.mult),
+                tt(c_r[:, sl], mn, rxn, ALU.mult),
+                ts(c_dn[:, sl], c_nv[:, sl], 1.0, None, ALU.add),
+                rcp(c_rdn[:, sl], c_dn[:, sl]),
+                ts(c_base[:, sl], c_rdn[:, sl], 2.0, -1.0, ALU.mult, ALU.add),
+                power(c_e[:, sl], c_base[:, sl], c_r[:, sl]),
+            ]
+            seg2 = [
+                ts(c_e1[:, sl], c_e[:, sl], 1.0, None, ALU.add),
+                rcp(c_re[:, sl], c_e1[:, sl]),
+                ts(c_t[:, sl], c_re[:, sl], -2.0, 1.0, ALU.mult, ALU.add),
+                tt(c_s[:, sl], c_t[:, sl], rmn, ALU.mult),
+                tt(c_x2[:, sl], c_t[:, sl], c_t[:, sl], ALU.mult),
+                tt(c_xy[:, sl], c_s[:, sl], pb[:, sl], ALU.mult),
+                ts(c_c1[:, sl], c_xy[:, sl], 2.0, 1.0, ALU.mult, ALU.add),
+                stt(c_den[:, sl], c_x2[:, sl], y2[:], c_c1[:, sl], ALU.mult, ALU.add),
+                stt(c_num[:, sl], c_x2[:, sl], ym1[:], c_c1[:, sl], ALU.add, ALU.add),
+                ts(c_denc[:, sl], c_den[:, sl], 1e-15, None, ALU.max),
+                stt(c_as[:, sl], c_c1[:, sl], y2[:], c_s[:, sl], ALU.add, ALU.mult),
+                rcp(c_rden[:, sl], c_denc[:, sl]),
+                tt(c_nn2[:, sl], c_num[:, sl], c_rden[:, sl], ALU.mult),
+                ts(c_nn2c[:, sl], c_nn2[:, sl], 1e-30, None, ALU.max),
+            ]
+            root2 = [act(c_nn[:, sl], c_nn2c[:, sl], ACT.Sqrt)]
+            seg3 = [
+                rcp(c_rnn[:, sl], c_nn[:, sl]),
+                ts(c_f[:, sl], c_rnn[:, sl], 0.999, 1.0, ALU.mult, ALU.min),
+                tt(c_rf[:, sl], c_rden[:, sl], c_f[:, sl], ALU.mult),
+                tt(al[:, sl], c_as[:, sl], c_rf[:, sl], ALU.mult),
+                stt(nbe[:, sl], c_x2[:, sl], 1.0, c_rf[:, sl], ALU.subtract, ALU.mult),
+            ]
+            return seg0, root1, seg1, seg2, root2, seg3
+
+        first_v = {}
+        mid_s = {}
+        late_v = {}
+        avail = [0] * NCH
+        a = 0
+        for n in GROUPS:
+            b = a + n
+            s01 = b // CH - 1 + 3
+            s_2 = s01 + (3 if n >= 32 else 2)
+            s_3 = s_2 + 1
+            seg0, root1, seg1, seg2, root2, seg3 = chain(a, b)
+            first_v[s01] = first_v.get(s01, []) + seg0
+            mid_s[s01] = mid_s.get(s01, []) + root1
+            late_v[s01] = late_v.get(s01, []) + seg1
+            late_v[s_2] = late_v.get(s_2, []) + seg2
+            mid_s[s_3] = mid_s.get(s_3, []) + root2
+            late_v[s_3] = late_v.get(s_3, []) + seg3
+            for c in range(a // CH, b // CH):
+                avail[c] = s_3 + 1
+            a = b
+        p2 = []
+        done = 0
+        while done < NCH:
+            s = len(p2)
+            cap = 1 if s < NCH else 2
+            now = []
+            while len(now) < cap and done < NCH and avail[done] <= s:
+                now.append(done)
+                done += 1
+            p2.append(now)
+        p2.append([])
+
+        make_identity(nc, ident[:])
+        v.memset(half[:], 0.5)
+        sc.dma_start(out=bias_bc[:], in_=bias.partition_broadcast(P))
+        load(0, 2)
+        nc.sync.dma_start(out=w_raw[:], in_=weight)
+        for blk in range(1, LOOKAHEAD):
+            load(blk, 1)
+        transposes(0)
+        w_bank = ps_ms.tile([P, 512], F32, name="ms")
+        w_words = w_raw[:].bitcast(F32)
+        for u in range(2):
+            nc.tensor.transpose(w_bank[:, u * P : (u + 1) * P], w_words[:, u * P : (u + 1) * P], ident[:])
+        v.tensor_scalar(out=u_f[:], in0=bias_bc[:], scalar1=0.1, scalar2=None, op0=ALU.mult)
+        sc.activation(out=junk_d[:], in_=u_f[:], func=ACT.Square, accum_out=un2[:])
+        first_v[0] = [
+            ts(un2c[:], un2[:], 1e-30, None, ALU.max),
+            power(un[:], un2c[:], half[:]),
+            ts(
+                w_grouped[:].rearrange("p (o u e) -> p o u e", u=2, e=2),
+                w_bank[:, 0 : 2 * P].bitcast(BF16).rearrange("p (u o e) -> p o u e", u=2, e=2),
+                0.1,
+                None,
+                ALU.mult,
+            ),
+            lambda: v.quantize_mx(out=w_codes[:].bitcast(FP8X4), scales=w_scales[:], in_=w_grouped[:]),
+            rcp(run[:], un[:]),
+        ]
+        mid_s[0] = [act(th[:], un[:], ACT.Tanh)]
+        late_v[0] = [
+            tt(kk[:], th[:], run[:], ALU.mult),
+            ts(b_pos[:], u_f[:], kk[:], None, ALU.mult),
+            ts(b_neg[:], u_f[:], kk[:], -1.0, ALU.mult, ALU.mult),
+        ]
+        mid_s[1] = [act(junk_d[:], b_pos[:], ACT.Square, y2[:])]
+        late_v[1] = [ts(ym1[:], y2[:], -1.0, None, ALU.add)]
+
+        for s in range(len(p2) - 1):
+            tail = s >= NCH
+            if s % 2 == 0 and s // 2 + LOOKAHEAD < NCH // 2:
+                load(s // 2 + LOOKAHEAD, 1)
+            if s < NCH:
+                copies(s, len(p2[s]))
+            for f in first_v.get(s, []):
+                f()
+            s_calls = []
+            if s < NCH:
+                s_calls += x_squares(s)
+            if 0 <= s - 2 < NCH:
+                s_calls += m_squares(s - 2)
+            if tail:
+                for c in p2[s]:
+                    s_calls += finish_scalar(c)
+            weave(s_calls[:1], [], 0)
+            for f in mid_s.get(s, []):
+                f()
+            weave(s_calls[1:], [], 0)
+            if 0 <= s - 1 < NCH:
+                quantise(s - 1)
+            if s + 1 < NCH:
+                transposes(s + 1)
+            if 0 <= s - 1 < NCH:
+                products(s - 1, ps_ms, "ms", ms_of)
+                products(s - 1, ps_mv, "mv", mv_of)
+            v_calls = []
+            if 0 <= s - 2 < NCH:
+                v_calls += m_dot_b(s - 2)
+            for c in p2[s]:
+                v_calls += finish_vector(c, tail)
+            weave(v_calls, late_v.get(s, []), 2)
+            for c in p2[s + 1]:
+                products(c, ps_m2, "m2", m2_of)

@@ -54,9 +54,9 @@ def tile_hypequalizedlinear_t_kernel(tc, x, weight, bias, out):
         half = col("half")
         w_raw = const.tile([P, K], BF16, name="w_raw")
         bias_bc = const.tile([P, DOUT], BF16, name="bias_bc")
-        junk_c = const.tile([P, K], BF16, name="junk_c")
-        junk_d = const.tile([P, DOUT], F32, name="junk_d")
-        junk_e = const.tile([P, DOUT], F32, name="junk_e")
+        junk_c = [const.tile([P, K], BF16, name="junk_c%d" % i) for i in range(4)]
+        junk_d = [const.tile([P, DOUT], F32, name="junk_d%d" % i) for i in range(4)]
+        junk_e = [const.tile([P, DOUT], F32, name="junk_e%d" % i) for i in range(4)]
         w_grouped = const.tile([P, K], BF16, name="w_grouped", align_bytes=64)
         w_codes = const.tile([P, DOUT], U32, name="w_codes", align_bytes=64)
         w_scales = const.tile([P, DOUT], U8, name="w_scales", align_bytes=64)
@@ -141,7 +141,7 @@ def tile_hypequalizedlinear_t_kernel(tc, x, weight, bias, out):
             i = 0
             for n, f in enumerate(bulk):
                 f()
-                if n >= skip and i < len(extra):
+                if n >= skip and n % 2 == 0 and i < len(extra):
                     extra[i]()
                     i += 1
             for f in extra[i:]:
@@ -198,7 +198,7 @@ def tile_hypequalizedlinear_t_kernel(tc, x, weight, bias, out):
             for j in range(CH):
                 loc = (c % 2) * CH + j
                 t = c * CH + j
-                calls.append(act(junk_c[:], xs[:, loc * K : (loc + 1) * K], ACT.Square, s2[:, 0, t : t + 1]))
+                calls.append(act(junk_c[j][:], xs[:, loc * K : (loc + 1) * K], ACT.Square, s2[:, 0, t : t + 1]))
             return calls
 
         def quantise(c):
@@ -217,14 +217,14 @@ def tile_hypequalizedlinear_t_kernel(tc, x, weight, bias, out):
 
         def m_squares(c):
             return [
-                act(junk_d[:], ms_of[c][:, j * P : (j + 1) * P], ACT.Square, s2[:, 1, c * CH + j : c * CH + j + 1])
+                act(junk_d[j][:], ms_of[c][:, j * P : (j + 1) * P], ACT.Square, s2[:, 1, c * CH + j : c * CH + j + 1])
                 for j in range(CH)
             ]
 
         def m_dot_b(c):
             return [
                 stt(
-                    junk_e[:],
+                    junk_e[j][:],
                     mv_of[c][:, j * P : (j + 1) * P],
                     1.0,
                     b_pos[:],
@@ -255,6 +255,7 @@ def tile_hypequalizedlinear_t_kernel(tc, x, weight, bias, out):
             y = y_of[c // 2]
             off = (c % 2) * CH * DOUT
             calls = []
+            first = []
             if with_scalar:
                 t1 = t1_of[c]
                 for j in range(CH):
@@ -273,7 +274,7 @@ def tile_hypequalizedlinear_t_kernel(tc, x, weight, bias, out):
                 bb = bpool.tile([P, CH * DOUT], F32, name="bb")
                 for j in range(CH):
                     t = c * CH + j
-                    calls.append(ts(bb[:, j * P : (j + 1) * P], b_neg[:], nbe[:, t : t + 1], None, ALU.mult))
+                    first.append(ts(bb[:, j * P : (j + 1) * P], b_neg[:], nbe[:, t : t + 1], None, ALU.mult))
                 for j in range(CH):
                     t = c * CH + j
                     calls.append(
@@ -287,10 +288,10 @@ def tile_hypequalizedlinear_t_kernel(tc, x, weight, bias, out):
                         )
                     )
             ysl = y[:, off : off + CH * DOUT]
-            calls.append(stt(ysl, ysl, 0.2, ysl, ALU.mult, ALU.max))
+            last = [stt(ysl, ysl, 0.2, ysl, ALU.mult, ALU.max)]
             if c % 2 == 1:
-                calls.append(store(c))
-            return calls
+                last.append(store(c))
+            return first, calls, last
 
         def chain(a, b):
             sl = slice(a, b)
@@ -380,7 +381,7 @@ def tile_hypequalizedlinear_t_kernel(tc, x, weight, bias, out):
         for u in range(2):
             nc.tensor.transpose(w_bank[:, u * P : (u + 1) * P], w_words[:, u * P : (u + 1) * P], ident[:])
         v.tensor_scalar(out=u_f[:], in0=bias_bc[:], scalar1=0.1, scalar2=None, op0=ALU.mult)
-        sc.activation(out=junk_d[:], in_=u_f[:], func=ACT.Square, accum_out=un2[:])
+        sc.activation(out=junk_d[0][:], in_=u_f[:], func=ACT.Square, accum_out=un2[:])
         first_v[0] = [
             ts(un2c[:], un2[:], 1e-30, None, ALU.max),
             power(un[:], un2c[:], half[:]),
@@ -400,9 +401,10 @@ def tile_hypequalizedlinear_t_kernel(tc, x, weight, bias, out):
             ts(b_pos[:], u_f[:], kk[:], None, ALU.mult),
             ts(b_neg[:], u_f[:], kk[:], -1.0, ALU.mult, ALU.mult),
         ]
-        mid_s[1] = [act(junk_d[:], b_pos[:], ACT.Square, y2[:])]
+        mid_s[1] = [act(junk_d[1][:], b_pos[:], ACT.Square, y2[:])]
         late_v[1] = [ts(ym1[:], y2[:], -1.0, None, ALU.add)]
 
+        pending = []
         for s in range(len(p2) - 1):
             tail = s >= NCH
             if s % 2 == 0 and s // 2 + LOOKAHEAD < NCH // 2:
@@ -431,10 +433,15 @@ def tile_hypequalizedlinear_t_kernel(tc, x, weight, bias, out):
                 products(s - 1, ps_ms, "ms", ms_of)
                 products(s - 1, ps_mv, "mv", mv_of)
             v_calls = []
-            if 0 <= s - 2 < NCH:
-                v_calls += m_dot_b(s - 2)
+            dots = m_dot_b(s - 2) if 0 <= s - 2 < NCH else []
             for c in p2[s]:
-                v_calls += finish_vector(c, tail)
+                first, second, last = finish_vector(c, tail)
+                v_calls += first + pending + dots + second
+                pending = last
+                dots = []
+            v_calls += dots
+            if s == len(p2) - 2:
+                v_calls += pending
             weave(v_calls, late_v.get(s, []), 2)
             for c in p2[s + 1]:
                 products(c, ps_m2, "m2", m2_of)

from contextlib import ExitStack

import concourse.mybir as mybir
from concourse.masks import make_identity

FLOPS = 2 * 16384 * 512 * 128

F32 = mybir.dt.float32
BF16 = mybir.dt.bfloat16
U32 = mybir.dt.uint32
U8 = mybir.dt.uint8
FP8X4 = mybir.dt.float8_e4m3fn_x4
ALU = mybir.AluOpType
ACT = mybir.ActivationFunctionType

P = 128
K = 512
DOUT = 128
NT = 128
CH = 4
NCH = NT // CH
GROUPS = (32, 32, 32, 16, 8, 8)
LOOKAHEAD = 4


def tile_hypequalizedlinear_t_kernel(tc, x, weight, bias, out):
    nc = tc.nc
    xv = x.rearrange("(p t) k -> p t k", t=NT)
    ov = out.rearrange("(p t) o -> p t o", t=NT)
    with ExitStack() as ctx:
        const = ctx.enter_context(tc.tile_pool(name="const", bufs=1))
        xpool = ctx.enter_context(tc.tile_pool(name="xpool", bufs=6))
        gpool = ctx.enter_context(tc.tile_pool(name="gpool", bufs=3))
        bpool = ctx.enter_context(tc.tile_pool(name="bpool", bufs=3))
        ypool = ctx.enter_context(tc.tile_pool(name="ypool", bufs=4))
        ps_xt = ctx.enter_context(tc.psum_pool(name="ps_xt", bufs=2))
        ps_ms = ctx.enter_context(tc.psum_pool(name="ps_ms", bufs=2))
        ps_mv = ctx.enter_context(tc.psum_pool(name="ps_mv", bufs=2))
        ps_m2 = ctx.enter_context(tc.psum_pool(name="ps_m2", bufs=2))

        ctx.enter_context(tc.manual_schedule())
        v = nc.vector
        sc = nc.scalar

        def col(name):
            return const.tile([P, 1], F32, name=name)

        def wide(name, n=1):
            if n == 1:
                return const.tile([P, NT], F32, name=name)
            return const.tile([P, n, NT], F32, name=name)

        ident = const.tile([P, P], F32, name="ident")
        half = col("half")
        w_raw = const.tile([P, K], BF16, name="w_raw")
        bias_bc = const.tile([P, DOUT], BF16, name="bias_bc")
        junk_c = [const.tile([P, K], BF16, name="junk_c%d" % i) for i in range(4)]
        junk_d = [const.tile([P, DOUT], F32, name="junk_d%d" % i) for i in range(4)]
        junk_e = [const.tile([P, DOUT], F32, name="junk_e%d" % i) for i in range(4)]
        w_grouped = const.tile([P, K], BF16, name="w_grouped", align_bytes=64)
        w_codes = const.tile([P, DOUT], U32, name="w_codes", align_bytes=64)
        w_scales = const.tile([P, DOUT], U8, name="w_scales", align_bytes=64)
        u_f = const.tile([P, DOUT], F32, name="u_f")
        b_pos = const.tile([P, DOUT], F32, name="b_pos")
        b_neg = const.tile([P, DOUT], F32, name="b_neg")
        un2 = col("un2")
        un2c = col("un2c")
        un = col("un")
        th = col("th")
        run = col("run")
        kk = col("kk")
        y2 = col("y2")
        ym1 = col("ym1")
        codes = const.tile([P, NT * P], U32, name="codes", align_bytes=64)
        scales = const.tile([P, NT * P], U8, name="scales", align_bytes=64)
        s2 = wide("s2", 2)
        pb = wide("pb")
        al = wide("al")
        nbe = wide("nbe")
        c_s2c = wide("c_s2c", 2)
        c_nrm = wide("c_nrm", 2)
        c_rnrm = wide("c_rnrm", 2)
        c_nv = wide("c_nv")
        c_dn = wide("c_dn")
        c_rdn = wide("c_rdn")
        c_base = wide("c_base")
        c_r = wide("c_r")
        c_e = wide("c_e")
        c_e1 = wide("c_e1")
        c_re = wide("c_re")
        c_t = wide("c_t")
        c_s = wide("c_s")
        c_x2 = wide("c_x2")
        c_xy = wide("c_xy")
        c_c1 = wide("c_c1")
        c_den = wide("c_den")
        c_denc = wide("c_denc")
        c_rden = wide("c_rden")
        c_num = wide("c_num")
        c_nn2 = wide("c_nn2")
        c_nn2c = wide("c_nn2c")
        c_nn = wide("c_nn")
        c_rnn = wide("c_rnn")
        c_f = wide("c_f")
        c_rf = wide("c_rf")
        c_as = wide("c_as")

        xs_of = {}
        xt_of = {}
        g_of = {}
        ms_of = {}
        mv_of = {}
        m2_of = {}
        t1_of = {}
        y_of = {}

        def ts(o, i, s1, s2_, o0, o1=None):
            if o1 is None:
                return lambda: v.tensor_scalar(out=o, in0=i, scalar1=s1, scalar2=None, op0=o0)
            return lambda: v.tensor_scalar(out=o, in0=i, scalar1=s1, scalar2=s2_, op0=o0, op1=o1)

        def tt(o, i0, i1, op):
            return lambda: v.tensor_tensor(out=o, in0=i0, in1=i1, op=op)

        def stt(o, i0, s, i1, o0, o1, acc=None):
            return lambda: v.scalar_tensor_tensor(out=o, in0=i0, scalar=s, in1=i1, op0=o0, op1=o1, accum_out=acc)

        def rcp(o, i):
            return lambda: v.reciprocal(out=o, in_=i)

        def act(o, i, func, acc=None):
            return lambda: sc.activation(out=o, in_=i, func=func, accum_out=acc)

        def scaled(o, i, s):
            return lambda: sc.activation(out=o, in_=i, func=ACT.Copy, scale=s)

        def power(o, i0, i1):
            return lambda: nc.gpsimd.tensor_tensor(out=o, in0=i0, in1=i1, op=ALU.pow)

        def weave(bulk, extra, skip):
            i = 0
            for n, f in enumerate(bulk):
                f()
                if n >= skip and n % 2 == 0 and i < len(extra):
                    extra[i]()
                    i += 1
            for f in extra[i:]:
                f()

        def mx(dst, t):
            nc.tensor.matmul_mx(
                out=dst,
                lhsT=codes[:, t * P : (t + 1) * P].bitcast(FP8X4),
                lhsT_scale=scales[:, t * P : (t + 1) * P],
                rhs=w_codes[:].bitcast(FP8X4),
                rhs_scale=w_scales[:],
                start=True,
                stop=True,
            )

        def load(blk, parts):
            xs = xpool.tile([P, 2 * CH * K], BF16, name="xs")
            xs_of[blk] = xs
            n = 2 * CH // parts
            for i in range(parts):
                nc.sync.dma_start(
                    out=xs[:, i * n * K : (i + 1) * n * K].rearrange("p (t k) -> p t k", k=K),
                    in_=xv[:, blk * 2 * CH + i * n : blk * 2 * CH + (i + 1) * n, :],
                )

        def transposes(c):
            xw = xs_of[c // 2][:].bitcast(F32)
            banks = []
            for h in range(2):
                xt = ps_xt.tile([P, 512], F32, name="xt")
                banks.append(xt)
                for q in range(4):
                    loc = (c % 2) * CH + 2 * h + q // 2
                    w0 = loc * (K // 2) + (q % 2) * P
                    nc.tensor.transpose(xt[:, q * P : (q + 1) * P], xw[:, w0 : w0 + P], ident[:])
            xt_of[c] = banks

        def copies(c, on_scalar):
            g = gpool.tile([P, CH * K], BF16, name="g", align_bytes=64)
            g_of[c] = g
            gw = g[:].bitcast(F32)
            for h in range(2):
                dst = gw[:, h * 512 : (h + 1) * 512].rearrange("p (t r u) -> p t r u", t=2, u=2)
                src = xt_of[c][h][:].rearrange("p (t u r) -> p t r u", t=2, u=2)
                if h >= 2 - on_scalar:
                    sc.copy(out=dst, in_=src)
                else:
                    v.tensor_copy(out=dst, in_=src)

        def x_squares(c):
            xs = xs_of[c // 2]
            calls = []
            for j in range(CH):
                loc = (c % 2) * CH + j
                t = c * CH + j
                calls.append(act(junk_c[j][:], xs[:, loc * K : (loc + 1) * K], ACT.Square, s2[:, 0, t : t + 1]))
            return calls

        def quantise(c):
            t0 = c * CH
            v.quantize_mx(
                out=codes[:, t0 * P : (t0 + CH) * P].bitcast(FP8X4),
                scales=scales[:, t0 * P : (t0 + CH) * P],
                in_=g_of[c][:],
            )

        def products(c, pool, name, keep):
            bank = pool.tile([P, 512], F32, name=name)
            keep[c] = bank
            for j in range(CH):
                mx(bank[:, j * P : (j + 1) * P], c * CH + j)

        def m_squares(c):
            return [
                act(junk_d[j][:], ms_of[c][:, j * P : (j + 1) * P], ACT.Square, s2[:, 1, c * CH + j : c * CH + j + 1])
                for j in range(CH)
            ]

        def m_dot_b(c):
            return [
                stt(
                    junk_e[j][:],
                    mv_of[c][:, j * P : (j + 1) * P],
                    1.0,
                    b_pos[:],
                    ALU.mult,
                    ALU.mult,
                    pb[:, c * CH + j : c * CH + j + 1],
                )
                for j in range(CH)
            ]

        def store(c):
            return lambda: nc.sync.dma_start(
                out=ov[:, (c - 1) * CH : (c + 1) * CH, :],
                in_=y_of[c // 2][:].rearrange("p (t o) -> p t o", o=DOUT),
            )

        def finish_scalar(c):
            t1 = bpool.tile([P, CH * DOUT], F32, name="bb")
            t1_of[c] = t1
            return [
                scaled(t1[:, j * P : (j + 1) * P], m2_of[c][:, j * P : (j + 1) * P], al[:, c * CH + j : c * CH + j + 1])
                for j in range(CH)
            ]

        def finish_vector(c, with_scalar):
            if c % 2 == 0:
                y_of[c // 2] = ypool.tile([P, 2 * CH * DOUT], F32, name="y")
            y = y_of[c // 2]
            off = (c % 2) * CH * DOUT
            calls = []
            first = []
            if with_scalar:
                t1 = t1_of[c]
                for j in range(CH):
                    t = c * CH + j
                    calls.append(
                        stt(
                            y[:, off + j * P : off + (j + 1) * P],
                            b_neg[:],
                            nbe[:, t : t + 1],
                            t1[:, j * P : (j + 1) * P],
                            ALU.mult,
                            ALU.add,
                        )
                    )
            else:
                bb = bpool.tile([P, CH * DOUT], F32, name="bb")
                for j in range(CH):
                    t = c * CH + j
                    first.append(ts(bb[:, j * P : (j + 1) * P], b_neg[:], nbe[:, t : t + 1], None, ALU.mult))
                for j in range(CH):
                    t = c * CH + j
                    calls.append(
                        stt(
                            y[:, off + j * P : off + (j + 1) * P],
                            m2_of[c][:, j * P : (j + 1) * P],
                            al[:, t : t + 1],
                            bb[:, j * P : (j + 1) * P],
                            ALU.mult,
                            ALU.add,
                        )
                    )
            ysl = y[:, off : off + CH * DOUT]
            last = [stt(ysl, ysl, 0.2, ysl, ALU.mult, ALU.max)]
            if c % 2 == 1:
                last.append(store(c))
            return first, calls, last

        def chain(a, b):
            sl = slice(a, b)
            xn = c_nrm[:, 0, sl]
            mn = c_nrm[:, 1, sl]
            rxn = c_rnrm[:, 0, sl]
            rmn = c_rnrm[:, 1, sl]
            seg0 = [ts(c_s2c[:, :, sl], s2[:, :, sl], 1e-30, None, ALU.max)]
            root1 = [act(c_nrm[:, :, sl], c_s2c[:, :, sl], ACT.Sqrt)]
            seg1 = [
                rcp(c_rnrm[:, :, sl], c_nrm[:, :, sl]),
                ts(c_nv[:, sl], xn, 1.0 - 1e-5, -1.0, ALU.min, ALU.mult),
                tt(c_r[:, sl], mn, rxn, ALU.mult),
                ts(c_dn[:, sl], c_nv[:, sl], 1.0, None, ALU.add),
                rcp(c_rdn[:, sl], c_dn[:, sl]),
                ts(c_base[:, sl], c_rdn[:, sl], 2.0, -1.0, ALU.mult, ALU.add),
                power(c_e[:, sl], c_base[:, sl], c_r[:, sl]),
            ]
            seg2 = [
                ts(c_e1[:, sl], c_e[:, sl], 1.0, None, ALU.add),
                rcp(c_re[:, sl], c_e1[:, sl]),
                ts(c_t[:, sl], c_re[:, sl], -2.0, 1.0, ALU.mult, ALU.add),
                tt(c_s[:, sl], c_t[:, sl], rmn, ALU.mult),
                tt(c_x2[:, sl], c_t[:, sl], c_t[:, sl], ALU.mult),
                tt(c_xy[:, sl], c_s[:, sl], pb[:, sl], ALU.mult),
                ts(c_c1[:, sl], c_xy[:, sl], 2.0, 1.0, ALU.mult, ALU.add),
                stt(c_den[:, sl], c_x2[:, sl], y2[:], c_c1[:, sl], ALU.mult, ALU.add),
                stt(c_num[:, sl], c_x2[:, sl], ym1[:], c_c1[:, sl], ALU.add, ALU.add),
                ts(c_denc[:, sl], c_den[:, sl], 1e-15, None, ALU.max),
                stt(c_as[:, sl], c_c1[:, sl], y2[:], c_s[:, sl], ALU.add, ALU.mult),
                rcp(c_rden[:, sl], c_denc[:, sl]),
                tt(c_nn2[:, sl], c_num[:, sl], c_rden[:, sl], ALU.mult),
                ts(c_nn2c[:, sl], c_nn2[:, sl], 1e-30, None, ALU.max),
            ]
            root2 = [act(c_nn[:, sl], c_nn2c[:, sl], ACT.Sqrt)]
            seg3 = [
                rcp(c_rnn[:, sl], c_nn[:, sl]),
                ts(c_f[:, sl], c_rnn[:, sl], 0.999, 1.0, ALU.mult, ALU.min),
                tt(c_rf[:, sl], c_rden[:, sl], c_f[:, sl], ALU.mult),
                tt(al[:, sl], c_as[:, sl], c_rf[:, sl], ALU.mult),
                stt(nbe[:, sl], c_x2[:, sl], 1.0, c_rf[:, sl], ALU.subtract, ALU.mult),
            ]
            return seg0, root1, seg1, seg2, root2, seg3

        first_v = {}
        mid_s = {}
        late_v = {}
        avail = [0] * NCH
        a = 0
        for n in GROUPS:
            b = a + n
            s01 = b // CH - 1 + 3
            s_2 = s01 + (3 if n >= 32 else 2)
            s_3 = s_2 + 1
            seg0, root1, seg1, seg2, root2, seg3 = chain(a, b)
            first_v[s01] = first_v.get(s01, []) + seg0
            mid_s[s01] = mid_s.get(s01, []) + root1
            late_v[s01] = late_v.get(s01, []) + seg1
            late_v[s_2] = late_v.get(s_2, []) + seg2
            mid_s[s_3] = mid_s.get(s_3, []) + root2
            late_v[s_3] = late_v.get(s_3, []) + seg3
            for c in range(a // CH, b // CH):
                avail[c] = s_3 + 1
            a = b
        p2 = []
        done = 0
        while done < NCH:
            s = len(p2)
            cap = 1 if s < NCH else 2
            now = []
            while len(now) < cap and done < NCH and avail[done] <= s:
                now.append(done)
                done += 1
            p2.append(now)
        p2.append([])

        make_identity(nc, ident[:])
        v.memset(half[:], 0.5)
        sc.dma_start(out=bias_bc[:], in_=bias.partition_broadcast(P))
        load(0, 2)
        nc.sync.dma_start(out=w_raw[:], in_=weight)
        for blk in range(1, LOOKAHEAD):
            load(blk, 1)
        transposes(0)
        w_bank = ps_ms.tile([P, 512], F32, name="ms")
        w_words = w_raw[:].bitcast(F32)
        for u in range(2):
            nc.tensor.transpose(w_bank[:, u * P : (u + 1) * P], w_words[:, u * P : (u + 1) * P], ident[:])
        v.tensor_scalar(out=u_f[:], in0=bias_bc[:], scalar1=0.1, scalar2=None, op0=ALU.mult)
        sc.activation(out=junk_d[0][:], in_=u_f[:], func=ACT.Square, accum_out=un2[:])
        first_v[0] = [
            ts(un2c[:], un2[:], 1e-30, None, ALU.max),
            power(un[:], un2c[:], half[:]),
            ts(
                w_grouped[:].rearrange("p (o u e) -> p o u e", u=2, e=2),
                w_bank[:, 0 : 2 * P].bitcast(BF16).rearrange("p (u o e) -> p o u e", u=2, e=2),
                0.1,
                None,
                ALU.mult,
            ),
            lambda: v.quantize_mx(out=w_codes[:].bitcast(FP8X4), scales=w_scales[:], in_=w_grouped[:]),
            rcp(run[:], un[:]),
        ]
        mid_s[0] = [act(th[:], un[:], ACT.Tanh)]
        late_v[0] = [
            tt(kk[:], th[:], run[:], ALU.mult),
            ts(b_pos[:], u_f[:], kk[:], None, ALU.mult),
            ts(b_neg[:], u_f[:], kk[:], -1.0, ALU.mult, ALU.mult),
        ]
        mid_s[1] = [act(junk_d[1][:], b_pos[:], ACT.Square, y2[:])]
        late_v[1] = [ts(ym1[:], y2[:], -1.0, None, ALU.add)]

        pending = []
        for s in range(len(p2) - 1):
            tail = s >= NCH
            if s % 2 == 0 and s // 2 + LOOKAHEAD < NCH // 2:
                load(s // 2 + LOOKAHEAD, 1)
            if s < NCH:
                copies(s, len(p2[s]))
            for f in first_v.get(s, []):
                f()
            s_calls = []
            if s < NCH:
                s_calls += x_squares(s)
            if 0 <= s - 2 < NCH:
                s_calls += m_squares(s - 2)
            if tail:
                for c in p2[s]:
                    s_calls += finish_scalar(c)
            weave(s_calls[:1], [], 0)
            for f in mid_s.get(s, []):
                f()
            weave(s_calls[1:], [], 0)
            if 0 <= s - 1 < NCH:
                quantise(s - 1)
            if s + 1 < NCH:
                transposes(s + 1)
            if 0 <= s - 1 < NCH:
                products(s - 1, ps_ms, "ms", ms_of)
                products(s - 1, ps_mv, "mv", mv_of)
            v_calls = []
            dots = m_dot_b(s - 2) if 0 <= s - 2 < NCH else []
            for c in p2[s]:
                first, second, last = finish_vector(c, tail)
                v_calls += first + pending + dots + second
                pending = last
                dots = []
            v_calls += dots
            if s == len(p2) - 2:
                v_calls += pending
            weave(v_calls, late_v.get(s, []), 2)
            for c in p2[s + 1]:
                products(c, ps_m2, "m2", m2_of)
